import numpy as np
import ml_dtypes


def mxq(x, axis, fmt="e4m3"):
    dtype, down = {"e4m3": (ml_dtypes.float8_e4m3fn, 7), "e5m2": (ml_dtypes.float8_e5m2, 14)}[fmt]
    v = np.moveaxis(np.asarray(x, np.float32).astype(ml_dtypes.bfloat16).astype(np.float64), axis, -1)
    blocks = v.reshape(v.shape[:-1] + (-1, 32))
    amax = np.abs(blocks).max(-1, keepdims=True)
    byte = np.maximum(np.where(amax > 0, np.frexp(amax)[1] - 1 + 127, 0) - down, 1)
    scale = np.exp2(byte - 127.0)
    codes = (blocks / scale).astype(np.float32).astype(dtype).astype(np.float64)
    return np.moveaxis((codes * scale).reshape(v.shape), -1, axis)


WIDE = False


def mx_kscale(k):
    if not WIDE:
        return np.ones(k)
    levels = np.array([10, -10, 5, -5, 0])
    a = np.random.permutation(np.resize(levels, k // 512 * 4)).reshape(k // 512, 4)
    idx = np.arange(k)
    return np.exp2(a[idx // 512, idx % 128 // 32])


BF16 = ml_dtypes.bfloat16


def bf(x):
    return np.asarray(x, np.float32).astype(BF16)


def f64(x):
    return np.asarray(x).astype(np.float64)


B, S, DIM, H, NOPE, ROPE, VHD, KV_RANK = 2, 256, 2048, 16, 128, 64, 128, 512
QKHD = NOPE + ROPE
HALF = ROPE // 2


def rope(u, cos, sin):
    ur = u.reshape(u.shape[:-1] + (HALF, 2))
    a, b = ur[..., 0], ur[..., 1]
    c = cos[None, :, None, :]
    s = sin[None, :, None, :]
    return np.stack([a * c - b * s, a * s + b * c], axis=-1).reshape(u.shape)


def setup_inputs():
    s = mx_kscale(DIM)
    inv_freq = 1.0 / 10000.0 ** (np.arange(0, ROPE, 2) / ROPE)
    ang = np.arange(S)[:, None] * inv_freq[None, :]
    return {"x": bf(np.random.standard_normal((B, S, DIM)) * s),
            "wq_w": bf(np.random.standard_normal((DIM, H * QKHD)) / np.sqrt(DIM) / s[:, None]),
            "wq_b": bf(np.random.standard_normal(H * QKHD) * 0.2),
            "cos": bf(np.cos(ang)), "sin": bf(np.sin(ang))}


def reference(x, wq_w, wq_b, cos, sin):
    q = (mxq(f64(x), 2, "e4m3") @ mxq(f64(wq_w), 0, "e4m3")) + f64(wq_b)
    q = q.reshape(B, S, H, QKHD)
    return np.concatenate([q[..., :NOPE], rope(q[..., NOPE:], f64(cos), f64(sin))], axis=-1)

@@ -1,0 +1,232 @@
+from contextlib import ExitStack
+
+import concourse.mybir as mybir
+from concourse.masks import make_identity
+
+F32 = mybir.dt.float32
+BF16 = mybir.dt.bfloat16
+U32 = mybir.dt.uint32
+U8 = mybir.dt.uint8
+FP8X4 = mybir.dt.float8_e4m3fn_x4
+ADD = mybir.AluOpType.add
+MULT = mybir.AluOpType.mult
+
+P = 128
+PACK = 4
+K_PASS = P * PACK
+TOKENS = 512
+DIM = 2048
+HEAD = 192
+NOPE = 128
+ROPE = 64
+PAIRS = ROPE // 2
+COLS = 16 * HEAD
+BANK = 512
+
+TOKEN_TILES = TOKENS // P
+PASSES = DIM // K_PASS
+BLOCKS = COLS // BANK
+UNITS = BLOCKS * PASSES
+BANKS = BLOCKS * TOKEN_TILES
+assert UNITS == BANKS
+
+FINISH_LAG = 5
+
+EARLY_UNITS = 2 * PASSES
+
+Q_WIDTH = BANK + NOPE
+
+FLOPS = 2 * TOKENS * DIM * COLS
+
+
+def tile_mla_pb_kernel(tc, x, wq_w, wq_b, cos, sin, out):
+    nc = tc.nc
+    x_rows = x.flatten_outer_dims()
+    out_rows = out.rearrange("b s h d -> (b s) (h d)")
+
+    with ExitStack() as stack:
+        const = stack.enter_context(tc.tile_pool(name="const", bufs=1))
+        x_pool = stack.enter_context(tc.tile_pool(name="x_pool", bufs=TOKEN_TILES))
+        raw_pool = stack.enter_context(tc.tile_pool(name="raw_pool", bufs=UNITS))
+        grouped_pool = stack.enter_context(tc.tile_pool(name="grouped_pool", bufs=4))
+        codes_pool = stack.enter_context(tc.tile_pool(name="codes_pool", bufs=6))
+        q_pool = stack.enter_context(tc.tile_pool(name="q_pool", bufs=6))
+        rot_pool = stack.enter_context(tc.tile_pool(name="rot_pool", bufs=3))
+        psum = stack.enter_context(tc.psum_pool(name="psum", bufs=8))
+
+        identity = const.tile([P, P], F32, name="identity")
+        make_identity(nc, identity[:])
+
+        stack.enter_context(tc.manual_schedule())
+
+        cos_sb = const.tile([P, 2, PAIRS], BF16, name="cos_sb")
+        sin_sb = const.tile([P, 2, PAIRS], BF16, name="sin_sb")
+        nc.scalar.dma_start(out=cos_sb[:], in_=cos.rearrange("(a p) j -> p a j", p=P))
+        nc.scalar.dma_start(out=sin_sb[:], in_=sin.rearrange("(a p) j -> p a j", p=P))
+
+        x_raw = []
+        for t in range(TOKEN_TILES):
+            x_tile = x_pool.tile([P, DIM], BF16, name="x_raw")
+            nc.sync.dma_start(out=x_tile[:], in_=x_rows[t * P : (t + 1) * P, :])
+            x_raw.append(x_tile)
+
+        bias_sb = const.tile([P, COLS], BF16, name="bias_sb")
+        w_raw = []
+        for u in range(UNITS):
+            b, g = divmod(u, PASSES)
+            w_tile = raw_pool.tile([P, PACK, BANK], BF16, name="w_raw")
+            nc.sync.dma_start(
+                out=w_tile[:],
+                in_=wq_w[g * K_PASS : (g + 1) * K_PASS, b * BANK : (b + 1) * BANK].rearrange(
+                    "(p j) c -> p j c", j=PACK
+                ),
+            )
+            w_raw.append(w_tile)
+            if u == PASSES - 1:
+                nc.sync.dma_start(out=bias_sb[:], in_=wq_b.partition_broadcast(P))
+
+        neg_sin = const.tile([P, 2, PAIRS], BF16, name="neg_sin")
+        nc.vector.tensor_scalar_mul(out=neg_sin[:], in0=sin_sb[:], scalar1=-1.0)
+
+        x_codes = []
+        x_scales = []
+        for t in range(TOKEN_TILES):
+            words = x_raw[t][:].bitcast(F32).rearrange("r (g p u) -> r g u p", g=PASSES, u=2)
+            x_grouped = x_pool.tile([P, PASSES * P * PACK], BF16, name="x_grouped", align_bytes=64)
+            grouped_words = x_grouped[:].bitcast(F32).rearrange(
+                "p (g r u) -> p g r u", g=PASSES, u=2
+            )
+            for half in range(2):
+                flipped = psum.tile([P, 2, 2, P], F32, name="flipped", tag="bank")
+                for gg in range(2):
+                    for u in range(2):
+                        nc.tensor.transpose(
+                            flipped[:, gg, u, :], words[:, 2 * half + gg, u, :], identity[:]
+                        )
+                nc.scalar.copy(
+                    out=grouped_words[:, 2 * half : 2 * half + 2],
+                    in_=flipped[:].rearrange("p g u r -> p g r u"),
+                )
+            codes = x_pool.tile([P, PASSES * P], U32, name="x_codes", align_bytes=64)
+            scales = x_pool.tile([P, PASSES * P], U8, name="x_scales", align_bytes=64)
+            nc.vector.quantize_mx(out=codes[:].bitcast(FP8X4), scales=scales[:], in_=x_grouped[:])
+            x_codes.append(codes)
+            x_scales.append(scales)
+
+        w_grouped = {}
+        w_codes = {}
+        w_scales = {}
+        acc = {}
+        q_tiles = {}
+        products = {}
+
+        def regroup(u):
+            grouped = grouped_pool.tile([P, BANK, PACK], BF16, name="w_grouped", align_bytes=64)
+            dst = grouped[:].rearrange("p (c i) j -> p c j i", i=4)
+            src = w_raw[u][:].rearrange("p j (c i) -> p c j i", i=4)
+            if (u < EARLY_UNITS and u % 2 == 1) or u == UNITS - 1:
+                nc.vector.tensor_copy(out=dst, in_=src)
+            else:
+                nc.scalar.copy(out=dst, in_=src)
+            w_grouped[u] = grouped
+
+        def quantise(u):
+            codes = codes_pool.tile([P, BANK], U32, name="w_codes", align_bytes=64)
+            scales = codes_pool.tile([P, BANK], U8, name="w_scales", align_bytes=64)
+            nc.vector.quantize_mx(
+                out=codes[:].bitcast(FP8X4),
+                scales=scales[:],
+                in_=w_grouped[u][:].rearrange("p c j -> p (c j)"),
+            )
+            w_codes[u] = codes
+            w_scales[u] = scales
+
+        def multiply(u):
+            b, g = divmod(u, PASSES)
+            for t in range(TOKEN_TILES):
+                if g == 0:
+                    acc[b * TOKEN_TILES + t] = psum.tile([P, BANK], F32, name="acc", tag="bank")
+                nc.tensor.matmul_mx(
+                    out=acc[b * TOKEN_TILES + t][:],
+                    lhsT=x_codes[t][:, g * P : (g + 1) * P].bitcast(FP8X4),
+                    lhsT_scale=x_scales[t][:, g * P : (g + 1) * P],
+                    rhs=w_codes[u][:].bitcast(FP8X4),
+                    rhs_scale=w_scales[u][:],
+                    start=(g == 0),
+                    stop=(g == PASSES - 1),
+                )
+
+        def rotated_view(f):
+            b = f // TOKEN_TILES
+            first = (NOPE - b * BANK) % HEAD
+            heads = (BANK - first + NOPE) // HEAD
+            view = q_tiles[f][:, first : first + heads * HEAD].rearrange(
+                "p (h d) -> p h d", d=HEAD
+            )
+            return heads, view[:, :, 0:ROPE].rearrange("p h (j e) -> p h j e", e=2)
+
+        def add_bias(f):
+            b = f // TOKEN_TILES
+            q_tile = q_pool.tile([P, Q_WIDTH], F32, name="q_tile")
+            nc.vector.tensor_tensor(
+                out=q_tile[:, 0:BANK],
+                in0=acc[f][:],
+                in1=bias_sb[:, b * BANK : (b + 1) * BANK],
+                op=ADD,
+            )
+            q_tiles[f] = q_tile
+
+        def rotation_products(f):
+            a = f % 2
+            heads, pairs = rotated_view(f)
+            by_cos = rot_pool.tile([P, 3, PAIRS, 2], F32, name="by_cos")
+            by_sin = rot_pool.tile([P, 2, 3, PAIRS], F32, name="by_sin")
+            nc.vector.tensor_tensor(
+                out=by_cos[:, 0:heads],
+                in0=pairs,
+                in1=cos_sb[:, a, :].unsqueeze(1).unsqueeze(3).to_broadcast([P, heads, PAIRS, 2]),
+                op=MULT,
+            )
+            nc.vector.tensor_tensor(
+                out=by_sin[:, 0, 0:heads, :],
+                in0=pairs[:, :, :, 1],
+                in1=neg_sin[:, a, :].unsqueeze(1).to_broadcast([P, heads, PAIRS]),
+                op=MULT,
+            )
+            nc.vector.tensor_tensor(
+                out=by_sin[:, 1, 0:heads, :],
+                in0=pairs[:, :, :, 0],
+                in1=sin_sb[:, a, :].unsqueeze(1).to_broadcast([P, heads, PAIRS]),
+                op=MULT,
+            )
+            products[f] = (by_cos, by_sin)
+
+        def rotation_sum_and_store(f):
+            b, t = divmod(f, TOKEN_TILES)
+            heads, pairs = rotated_view(f)
+            by_cos, by_sin = products[f]
+            nc.vector.tensor_tensor(
+                out=pairs,
+                in0=by_cos[:, 0:heads],
+                in1=by_sin[:, :, 0:heads, :].rearrange("p e h j -> p h j e"),
+                op=ADD,
+            )
+            nc.sync.dma_start(
+                out=out_rows[t * P : (t + 1) * P, b * BANK : (b + 1) * BANK],
+                in_=q_tiles[f][:, 0:BANK],
+            )
+
+        regroup(0)
+        for step in range(UNITS + FINISH_LAG + 1):
+            f = step - FINISH_LAG
+            if step + 1 < UNITS:
+                regroup(step + 1)
+            if 0 <= f < BANKS:
+                add_bias(f)
+            if 0 <= f - 1 < BANKS:
+                rotation_sum_and_store(f - 1)
+            if step < UNITS:
+                quantise(step)
+                multiply(step)
+            if 0 <= f < BANKS:
+                rotation_products(f)

@@ -27,16 +27,21 @@ TOKEN_TILES = TOKENS // P
 PASSES = DIM // K_PASS
 BLOCKS = COLS // BANK
 UNITS = BLOCKS * PASSES
-BANKS = BLOCKS * TOKEN_TILES
-assert UNITS == BANKS
 
-FINISH_LAG = 5
-
-EARLY_UNITS = 2 * PASSES
-
+MAX_HEADS = 3
 Q_WIDTH = BANK + NOPE
 
+BLOCKS_AHEAD = 4
+VECTOR_COLUMNS = 256
+
 FLOPS = 2 * TOKENS * DIM * COLS
+
+
+def vector_columns(u):
+    b, g = divmod(u, PASSES)
+    if b == 0:
+        return BANK * (g % 2)
+    return VECTOR_COLUMNS if g == PASSES - 1 else 0
 
 
 def tile_mla_pb_kernel(tc, x, wq_w, wq_b, cos, sin, out):
@@ -47,17 +52,31 @@ def tile_mla_pb_kernel(tc, x, wq_w, wq_b, cos, sin, out):
     with ExitStack() as stack:
         const = stack.enter_context(tc.tile_pool(name="const", bufs=1))
         x_pool = stack.enter_context(tc.tile_pool(name="x_pool", bufs=TOKEN_TILES))
-        raw_pool = stack.enter_context(tc.tile_pool(name="raw_pool", bufs=UNITS))
+        raw_pool = stack.enter_context(tc.tile_pool(name="raw_pool", bufs=BLOCKS_AHEAD * PASSES))
         grouped_pool = stack.enter_context(tc.tile_pool(name="grouped_pool", bufs=4))
         codes_pool = stack.enter_context(tc.tile_pool(name="codes_pool", bufs=6))
-        q_pool = stack.enter_context(tc.tile_pool(name="q_pool", bufs=6))
-        rot_pool = stack.enter_context(tc.tile_pool(name="rot_pool", bufs=3))
+        q_pool = stack.enter_context(tc.tile_pool(name="q_pool", bufs=2))
         psum = stack.enter_context(tc.psum_pool(name="psum", bufs=8))
 
         identity = const.tile([P, P], F32, name="identity")
         make_identity(nc, identity[:])
 
         stack.enter_context(tc.manual_schedule())
+
+        w_raw = {}
+
+        def load_block(b):
+            for g in range(PASSES):
+                w_tile = raw_pool.tile([P, PACK, BANK], BF16, name="w_raw")
+                for u in range(2):
+                    first_row = g * K_PASS + u * 2 * P
+                    nc.sync.dma_start(
+                        out=w_tile[:, 2 * u : 2 * u + 2, :],
+                        in_=wq_w[
+                            first_row : first_row + 2 * P, b * BANK : (b + 1) * BANK
+                        ].rearrange("(p e) c -> p e c", e=2),
+                    )
+                w_raw[b * PASSES + g] = w_tile
 
         cos_sb = const.tile([P, 2, PAIRS], BF16, name="cos_sb")
         sin_sb = const.tile([P, 2, PAIRS], BF16, name="sin_sb")
@@ -70,67 +89,80 @@ def tile_mla_pb_kernel(tc, x, wq_w, wq_b, cos, sin, out):
             nc.sync.dma_start(out=x_tile[:], in_=x_rows[t * P : (t + 1) * P, :])
             x_raw.append(x_tile)
 
+        load_block(0)
         bias_sb = const.tile([P, COLS], BF16, name="bias_sb")
-        w_raw = []
-        for u in range(UNITS):
-            b, g = divmod(u, PASSES)
-            w_tile = raw_pool.tile([P, PACK, BANK], BF16, name="w_raw")
-            nc.sync.dma_start(
-                out=w_tile[:],
-                in_=wq_w[g * K_PASS : (g + 1) * K_PASS, b * BANK : (b + 1) * BANK].rearrange(
-                    "(p j) c -> p j c", j=PACK
-                ),
-            )
-            w_raw.append(w_tile)
-            if u == PASSES - 1:
-                nc.sync.dma_start(out=bias_sb[:], in_=wq_b.partition_broadcast(P))
+        nc.sync.dma_start(out=bias_sb[:], in_=wq_b.partition_broadcast(P))
+        for b in range(1, BLOCKS_AHEAD):
+            load_block(b)
 
-        neg_sin = const.tile([P, 2, PAIRS], BF16, name="neg_sin")
-        nc.vector.tensor_scalar_mul(out=neg_sin[:], in0=sin_sb[:], scalar1=-1.0)
+        cos_table = const.tile([P, 2, MAX_HEADS, PAIRS, 2], BF16, name="cos_table")
+        sin_table = const.tile([P, 2, 2, MAX_HEADS, PAIRS], BF16, name="sin_table")
+        nc.vector.tensor_copy(
+            out=cos_table[:],
+            in_=cos_sb[:].unsqueeze(2).unsqueeze(4).to_broadcast([P, 2, MAX_HEADS, PAIRS, 2]),
+        )
+        sin_heads = sin_sb[:].unsqueeze(2).to_broadcast([P, 2, MAX_HEADS, PAIRS])
+        nc.vector.tensor_scalar_mul(out=sin_table[:, 0], in0=sin_heads, scalar1=-1.0)
+        nc.vector.tensor_copy(out=sin_table[:, 1], in_=sin_heads)
 
+        x_grouped = []
         x_codes = []
         x_scales = []
-        for t in range(TOKEN_TILES):
-            words = x_raw[t][:].bitcast(F32).rearrange("r (g p u) -> r g u p", g=PASSES, u=2)
-            x_grouped = x_pool.tile([P, PASSES * P * PACK], BF16, name="x_grouped", align_bytes=64)
-            grouped_words = x_grouped[:].bitcast(F32).rearrange(
+
+        def x_flip(t):
+            words = x_raw[t][:].bitcast(F32)
+            grouped = x_pool.tile([P, PASSES * P * PACK], BF16, name="x_grouped", align_bytes=64)
+            grouped_words = grouped[:].bitcast(F32).rearrange(
                 "p (g r u) -> p g r u", g=PASSES, u=2
             )
             for half in range(2):
                 flipped = psum.tile([P, 2, 2, P], F32, name="flipped", tag="bank")
                 for gg in range(2):
                     for u in range(2):
+                        first_word = ((2 * half + gg) * 2 + u) * P
                         nc.tensor.transpose(
-                            flipped[:, gg, u, :], words[:, 2 * half + gg, u, :], identity[:]
+                            flipped[:, gg, u, :], words[:, first_word : first_word + P], identity[:]
                         )
                 nc.scalar.copy(
                     out=grouped_words[:, 2 * half : 2 * half + 2],
                     in_=flipped[:].rearrange("p g u r -> p g r u"),
                 )
+            x_grouped.append(grouped)
+
+        def x_quantise(t):
             codes = x_pool.tile([P, PASSES * P], U32, name="x_codes", align_bytes=64)
             scales = x_pool.tile([P, PASSES * P], U8, name="x_scales", align_bytes=64)
-            nc.vector.quantize_mx(out=codes[:].bitcast(FP8X4), scales=scales[:], in_=x_grouped[:])
+            nc.vector.quantize_mx(
+                out=codes[:].bitcast(FP8X4), scales=scales[:], in_=x_grouped[t][:]
+            )
             x_codes.append(codes)
             x_scales.append(scales)
 
+        for t in range(TOKEN_TILES):
+            x_flip(t)
+            x_quantise(t)
+
         w_grouped = {}
-        w_codes = {}
-        w_scales = {}
         acc = {}
-        q_tiles = {}
-        products = {}
 
         def regroup(u):
             grouped = grouped_pool.tile([P, BANK, PACK], BF16, name="w_grouped", align_bytes=64)
-            dst = grouped[:].rearrange("p (c i) j -> p c j i", i=4)
-            src = w_raw[u][:].rearrange("p j (c i) -> p c j i", i=4)
-            if (u < EARLY_UNITS and u % 2 == 1) or u == UNITS - 1:
-                nc.vector.tensor_copy(out=dst, in_=src)
-            else:
-                nc.scalar.copy(out=dst, in_=src)
+            split = BANK - vector_columns(u)
+            if split > 0:
+                nc.scalar.copy(
+                    out=grouped[:, 0:split, :].rearrange("p (c i) j -> p c j i", i=4),
+                    in_=w_raw[u][:, :, 0:split].rearrange("p j (c i) -> p c j i", i=4),
+                )
+            if split < BANK:
+                nc.vector.tensor_copy(
+                    out=grouped[:, split:BANK, :].rearrange("p (c i) j -> p c j i", i=4),
+                    in_=w_raw[u][:, :, split:BANK].rearrange("p j (c i) -> p c j i", i=4),
+                )
             w_grouped[u] = grouped
 
-        def quantise(u):
+        def prepare(u):
+            if u + 1 < UNITS:
+                regroup(u + 1)
             codes = codes_pool.tile([P, BANK], U32, name="w_codes", align_bytes=64)
             scales = codes_pool.tile([P, BANK], U8, name="w_scales", align_bytes=64)
             nc.vector.quantize_mx(
@@ -138,95 +170,89 @@ def tile_mla_pb_kernel(tc, x, wq_w, wq_b, cos, sin, out):
                 scales=scales[:],
                 in_=w_grouped[u][:].rearrange("p c j -> p (c j)"),
             )
-            w_codes[u] = codes
-            w_scales[u] = scales
-
-        def multiply(u):
             b, g = divmod(u, PASSES)
             for t in range(TOKEN_TILES):
                 if g == 0:
-                    acc[b * TOKEN_TILES + t] = psum.tile([P, BANK], F32, name="acc", tag="bank")
+                    acc[(b, t)] = psum.tile([P, BANK], F32, name="acc", tag="bank")
                 nc.tensor.matmul_mx(
-                    out=acc[b * TOKEN_TILES + t][:],
+                    out=acc[(b, t)][:],
                     lhsT=x_codes[t][:, g * P : (g + 1) * P].bitcast(FP8X4),
                     lhsT_scale=x_scales[t][:, g * P : (g + 1) * P],
-                    rhs=w_codes[u][:].bitcast(FP8X4),
-                    rhs_scale=w_scales[u][:],
+                    rhs=codes[:].bitcast(FP8X4),
+                    rhs_scale=scales[:],
                     start=(g == 0),
                     stop=(g == PASSES - 1),
                 )
 
-        def rotated_view(f):
-            b = f // TOKEN_TILES
+        q_tiles = {}
+        products = {}
+
+        def add_bias(b):
+            q_tile = q_pool.tile([P, TOKEN_TILES, Q_WIDTH], F32, name="q_tile")
+            for t in range(TOKEN_TILES):
+                nc.vector.tensor_tensor(
+                    out=q_tile[:, t, 0:BANK],
+                    in0=acc[(b, t)][:],
+                    in1=bias_sb[:, b * BANK : (b + 1) * BANK],
+                    op=ADD,
+                )
+            q_tiles[b] = q_tile
+
+        def rotated_view(b):
             first = (NOPE - b * BANK) % HEAD
             heads = (BANK - first + NOPE) // HEAD
-            view = q_tiles[f][:, first : first + heads * HEAD].rearrange(
-                "p (h d) -> p h d", d=HEAD
+            view = q_tiles[b][:, :, first : first + heads * HEAD].rearrange(
+                "p (s a) (h d) -> p s a h d", a=2, d=HEAD
             )
-            return heads, view[:, :, 0:ROPE].rearrange("p h (j e) -> p h j e", e=2)
+            return heads, view[:, :, :, :, 0:ROPE].rearrange("p s a h (j e) -> p s a h j e", e=2)
 
-        def add_bias(f):
-            b = f // TOKEN_TILES
-            q_tile = q_pool.tile([P, Q_WIDTH], F32, name="q_tile")
+        def rotation_products(b):
+            heads, pairs = rotated_view(b)
+            by_cos = q_pool.tile([P, 2, 2, MAX_HEADS, PAIRS, 2], F32, name="by_cos")
+            by_sin = q_pool.tile([P, 2, 2, 2, MAX_HEADS, PAIRS], F32, name="by_sin")
             nc.vector.tensor_tensor(
-                out=q_tile[:, 0:BANK],
-                in0=acc[f][:],
-                in1=bias_sb[:, b * BANK : (b + 1) * BANK],
-                op=ADD,
-            )
-            q_tiles[f] = q_tile
-
-        def rotation_products(f):
-            a = f % 2
-            heads, pairs = rotated_view(f)
-            by_cos = rot_pool.tile([P, 3, PAIRS, 2], F32, name="by_cos")
-            by_sin = rot_pool.tile([P, 2, 3, PAIRS], F32, name="by_sin")
-            nc.vector.tensor_tensor(
-                out=by_cos[:, 0:heads],
+                out=by_cos[:, :, :, 0:heads],
                 in0=pairs,
-                in1=cos_sb[:, a, :].unsqueeze(1).unsqueeze(3).to_broadcast([P, heads, PAIRS, 2]),
+                in1=cos_table[:, :, 0:heads].unsqueeze(1).to_broadcast([P, 2, 2, heads, PAIRS, 2]),
                 op=MULT,
             )
-            nc.vector.tensor_tensor(
-                out=by_sin[:, 0, 0:heads, :],
-                in0=pairs[:, :, :, 1],
-                in1=neg_sin[:, a, :].unsqueeze(1).to_broadcast([P, heads, PAIRS]),
-                op=MULT,
-            )
-            nc.vector.tensor_tensor(
-                out=by_sin[:, 1, 0:heads, :],
-                in0=pairs[:, :, :, 0],
-                in1=sin_sb[:, a, :].unsqueeze(1).to_broadcast([P, heads, PAIRS]),
-                op=MULT,
-            )
-            products[f] = (by_cos, by_sin)
+            for e in range(2):
+                nc.vector.tensor_tensor(
+                    out=by_sin[:, e, :, :, 0:heads, :],
+                    in0=pairs[:, :, :, :, :, 1 - e],
+                    in1=sin_table[:, e, :, 0:heads, :]
+                    .unsqueeze(1)
+                    .to_broadcast([P, 2, 2, heads, PAIRS]),
+                    op=MULT,
+                )
+            products[b] = (by_cos, by_sin)
 
-        def rotation_sum_and_store(f):
-            b, t = divmod(f, TOKEN_TILES)
-            heads, pairs = rotated_view(f)
-            by_cos, by_sin = products[f]
+        def rotation_sum_and_store(b):
+            heads, pairs = rotated_view(b)
+            by_cos, by_sin = products[b]
             nc.vector.tensor_tensor(
                 out=pairs,
-                in0=by_cos[:, 0:heads],
-                in1=by_sin[:, :, 0:heads, :].rearrange("p e h j -> p h j e"),
+                in0=by_cos[:, :, :, 0:heads],
+                in1=by_sin[:, :, :, :, 0:heads, :].rearrange("p e s a h j -> p s a h j e"),
                 op=ADD,
             )
             nc.sync.dma_start(
-                out=out_rows[t * P : (t + 1) * P, b * BANK : (b + 1) * BANK],
-                in_=q_tiles[f][:, 0:BANK],
+                out=out_rows[:, b * BANK : (b + 1) * BANK].rearrange("(t p) c -> p t c", p=P),
+                in_=q_tiles[b][:, :, 0:BANK],
             )
 
         regroup(0)
-        for step in range(UNITS + FINISH_LAG + 1):
-            f = step - FINISH_LAG
-            if step + 1 < UNITS:
-                regroup(step + 1)
-            if 0 <= f < BANKS:
-                add_bias(f)
-            if 0 <= f - 1 < BANKS:
-                rotation_sum_and_store(f - 1)
-            if step < UNITS:
-                quantise(step)
-                multiply(step)
-            if 0 <= f < BANKS:
-                rotation_products(f)
+        for b in range(BLOCKS + 1):
+            if 1 <= b and b - 1 + BLOCKS_AHEAD < BLOCKS:
+                load_block(b - 1 + BLOCKS_AHEAD)
+            if b >= 1:
+                add_bias(b - 1)
+            if b < BLOCKS:
+                prepare(b * PASSES)
+            if b >= 1:
+                rotation_products(b - 1)
+            if b < BLOCKS:
+                for g in range(1, PASSES):
+                    prepare(b * PASSES + g)
+            if b >= 1:
+                rotation_sum_and_store(b - 1)

@@ -78,6 +78,11 @@ def tile_mla_pb_kernel(tc, x, wq_w, wq_b, cos, sin, out):
                     )
                 w_raw[b * PASSES + g] = w_tile
 
+        bias_row = const.tile([P, COLS], BF16, name="bias_row")
+        ones = const.tile([P, P], BF16, name="ones")
+        nc.vector.memset(bias_row[:].bitcast(F32), 0.0)
+        nc.vector.memset(ones[:], 1.0)
+        nc.scalar.dma_start(out=bias_row[0:1, :], in_=wq_b.unsqueeze(0))
         cos_sb = const.tile([P, 2, PAIRS], BF16, name="cos_sb")
         sin_sb = const.tile([P, 2, PAIRS], BF16, name="sin_sb")
         nc.scalar.dma_start(out=cos_sb[:], in_=cos.rearrange("(a p) j -> p a j", p=P))
@@ -89,11 +94,20 @@ def tile_mla_pb_kernel(tc, x, wq_w, wq_b, cos, sin, out):
             nc.sync.dma_start(out=x_tile[:], in_=x_rows[t * P : (t + 1) * P, :])
             x_raw.append(x_tile)
 
-        load_block(0)
-        bias_sb = const.tile([P, COLS], BF16, name="bias_sb")
-        nc.sync.dma_start(out=bias_sb[:], in_=wq_b.partition_broadcast(P))
-        for b in range(1, BLOCKS_AHEAD):
+        for b in range(BLOCKS_AHEAD):
             load_block(b)
+
+        bias_sb = const.tile([P, COLS], F32, name="bias_sb")
+        for c in range(BLOCKS):
+            spread = psum.tile([P, BANK], F32, name="spread", tag="bank")
+            nc.tensor.matmul(
+                out=spread[:],
+                lhsT=ones[:],
+                rhs=bias_row[:, c * BANK : (c + 1) * BANK],
+                start=True,
+                stop=True,
+            )
+            nc.vector.tensor_copy(out=bias_sb[:, c * BANK : (c + 1) * BANK], in_=spread[:])
 
         cos_table = const.tile([P, 2, MAX_HEADS, PAIRS, 2], BF16, name="cos_table")
         sin_table = const.tile([P, 2, 2, MAX_HEADS, PAIRS], BF16, name="sin_table")

@@ -55,7 +55,7 @@ def tile_mla_pb_kernel(tc, x, wq_w, wq_b, cos, sin, out):
         raw_pool = stack.enter_context(tc.tile_pool(name="raw_pool", bufs=BLOCKS_AHEAD * PASSES))
         grouped_pool = stack.enter_context(tc.tile_pool(name="grouped_pool", bufs=4))
         codes_pool = stack.enter_context(tc.tile_pool(name="codes_pool", bufs=6))
-        q_pool = stack.enter_context(tc.tile_pool(name="q_pool", bufs=2))
+        q_pool = stack.enter_context(tc.tile_pool(name="q_pool", bufs=3))
         psum = stack.enter_context(tc.psum_pool(name="psum", bufs=8))
 
         identity = const.tile([P, P], F32, name="identity")
@@ -259,14 +259,16 @@ def tile_mla_pb_kernel(tc, x, wq_w, wq_b, cos, sin, out):
         for b in range(BLOCKS + 1):
             if 1 <= b and b - 1 + BLOCKS_AHEAD < BLOCKS:
                 load_block(b - 1 + BLOCKS_AHEAD)
-            if b >= 1:
-                add_bias(b - 1)
             if b < BLOCKS:
                 prepare(b * PASSES)
             if b >= 1:
+                add_bias(b - 1)
+            if b < BLOCKS:
+                prepare(b * PASSES + 1)
+            if b >= 1:
                 rotation_products(b - 1)
             if b < BLOCKS:
-                for g in range(1, PASSES):
-                    prepare(b * PASSES + g)
+                prepare(b * PASSES + 2)
+                prepare(b * PASSES + 3)
             if b >= 1:
                 rotation_sum_and_store(b - 1)

@@ -32,9 +32,13 @@ MAX_HEADS = 3
 Q_WIDTH = BANK + NOPE
 
 BLOCKS_AHEAD = 4
-VECTOR_COLUMNS = 256
+VECTOR_COLUMNS = 128
 
 FLOPS = 2 * TOKENS * DIM * COLS
+
+
+def first_column(b):
+    return (BLOCKS - 1 - b) * BANK
 
 
 def vector_columns(u):
@@ -60,6 +64,8 @@ def tile_mla_pb_kernel(tc, x, wq_w, wq_b, cos, sin, out):
 
         identity = const.tile([P, P], F32, name="identity")
         make_identity(nc, identity[:])
+        identity_bf = const.tile([P, P], BF16, name="identity_bf")
+        make_identity(nc, identity_bf[:])
 
         stack.enter_context(tc.manual_schedule())
 
@@ -73,16 +79,14 @@ def tile_mla_pb_kernel(tc, x, wq_w, wq_b, cos, sin, out):
                     nc.sync.dma_start(
                         out=w_tile[:, 2 * u : 2 * u + 2, :],
                         in_=wq_w[
-                            first_row : first_row + 2 * P, b * BANK : (b + 1) * BANK
+                            first_row : first_row + 2 * P, first_column(b) : first_column(b) + BANK
                         ].rearrange("(p e) c -> p e c", e=2),
                     )
                 w_raw[b * PASSES + g] = w_tile
 
-        bias_row = const.tile([P, COLS], BF16, name="bias_row")
-        ones = const.tile([P, P], BF16, name="ones")
-        nc.vector.memset(bias_row[:].bitcast(F32), 0.0)
-        nc.vector.memset(ones[:], 1.0)
-        nc.scalar.dma_start(out=bias_row[0:1, :], in_=wq_b.unsqueeze(0))
+        bias_rows = const.tile([P, BANK], BF16, name="bias_rows")
+        nc.vector.memset(bias_rows[:].bitcast(F32), 0.0)
+        nc.sync.dma_start(out=bias_rows[0:BLOCKS, :], in_=wq_b.rearrange("(c n) -> c n", n=BANK))
         cos_sb = const.tile([P, 2, PAIRS], BF16, name="cos_sb")
         sin_sb = const.tile([P, 2, PAIRS], BF16, name="sin_sb")
         nc.scalar.dma_start(out=cos_sb[:], in_=cos.rearrange("(a p) j -> p a j", p=P))
@@ -98,26 +102,17 @@ def tile_mla_pb_kernel(tc, x, wq_w, wq_b, cos, sin, out):
             load_block(b)
 
         bias_sb = const.tile([P, COLS], F32, name="bias_sb")
-        for c in range(BLOCKS):
+
+        def spread_bias(c):
             spread = psum.tile([P, BANK], F32, name="spread", tag="bank")
             nc.tensor.matmul(
                 out=spread[:],
-                lhsT=ones[:],
-                rhs=bias_row[:, c * BANK : (c + 1) * BANK],
+                lhsT=identity_bf[:, c : c + 1].to_broadcast([P, P]),
+                rhs=bias_rows[:],
                 start=True,
                 stop=True,
             )
             nc.vector.tensor_copy(out=bias_sb[:, c * BANK : (c + 1) * BANK], in_=spread[:])
-
-        cos_table = const.tile([P, 2, MAX_HEADS, PAIRS, 2], BF16, name="cos_table")
-        sin_table = const.tile([P, 2, 2, MAX_HEADS, PAIRS], BF16, name="sin_table")
-        nc.vector.tensor_copy(
-            out=cos_table[:],
-            in_=cos_sb[:].unsqueeze(2).unsqueeze(4).to_broadcast([P, 2, MAX_HEADS, PAIRS, 2]),
-        )
-        sin_heads = sin_sb[:].unsqueeze(2).to_broadcast([P, 2, MAX_HEADS, PAIRS])
-        nc.vector.tensor_scalar_mul(out=sin_table[:, 0], in0=sin_heads, scalar1=-1.0)
-        nc.vector.tensor_copy(out=sin_table[:, 1], in_=sin_heads)
 
         x_grouped = []
         x_codes = []
@@ -153,8 +148,20 @@ def tile_mla_pb_kernel(tc, x, wq_w, wq_b, cos, sin, out):
             x_scales.append(scales)
 
         for t in range(TOKEN_TILES):
+            for c in range(2 * t, min(2 * t + 2, BLOCKS)):
+                spread_bias(c)
             x_flip(t)
             x_quantise(t)
+
+        cos_table = const.tile([P, 2, MAX_HEADS, PAIRS, 2], BF16, name="cos_table")
+        sin_table = const.tile([P, 2, 2, MAX_HEADS, PAIRS], BF16, name="sin_table")
+        nc.vector.tensor_copy(
+            out=cos_table[:],
+            in_=cos_sb[:].unsqueeze(2).unsqueeze(4).to_broadcast([P, 2, MAX_HEADS, PAIRS, 2]),
+        )
+        sin_heads = sin_sb[:].unsqueeze(2).to_broadcast([P, 2, MAX_HEADS, PAIRS])
+        nc.vector.tensor_scalar_mul(out=sin_table[:, 0], in0=sin_heads, scalar1=-1.0)
+        nc.vector.tensor_copy(out=sin_table[:, 1], in_=sin_heads)
 
         w_grouped = {}
         acc = {}
@@ -207,13 +214,13 @@ def tile_mla_pb_kernel(tc, x, wq_w, wq_b, cos, sin, out):
                 nc.vector.tensor_tensor(
                     out=q_tile[:, t, 0:BANK],
                     in0=acc[(b, t)][:],
-                    in1=bias_sb[:, b * BANK : (b + 1) * BANK],
+                    in1=bias_sb[:, first_column(b) : first_column(b) + BANK],
                     op=ADD,
                 )
             q_tiles[b] = q_tile
 
         def rotated_view(b):
-            first = (NOPE - b * BANK) % HEAD
+            first = (NOPE - first_column(b)) % HEAD
             heads = (BANK - first + NOPE) // HEAD
             view = q_tiles[b][:, :, first : first + heads * HEAD].rearrange(
                 "p (s a) (h d) -> p s a h d", a=2, d=HEAD
@@ -251,7 +258,9 @@ def tile_mla_pb_kernel(tc, x, wq_w, wq_b, cos, sin, out):
                 op=ADD,
             )
             nc.sync.dma_start(
-                out=out_rows[:, b * BANK : (b + 1) * BANK].rearrange("(t p) c -> p t c", p=P),
+                out=out_rows[:, first_column(b) : first_column(b) + BANK].rearrange(
+                    "(t p) c -> p t c", p=P
+                ),
                 in_=q_tiles[b][:, :, 0:BANK],
             )
 

@@ -32,20 +32,12 @@ MAX_HEADS = 3
 Q_WIDTH = BANK + NOPE
 
 BLOCKS_AHEAD = 4
-VECTOR_COLUMNS = 128
 
 FLOPS = 2 * TOKENS * DIM * COLS
 
 
 def first_column(b):
     return (BLOCKS - 1 - b) * BANK
-
-
-def vector_columns(u):
-    b, g = divmod(u, PASSES)
-    if b == 0:
-        return BANK * (g % 2)
-    return VECTOR_COLUMNS if g == PASSES - 1 else 0
 
 
 def tile_mla_pb_kernel(tc, x, wq_w, wq_b, cos, sin, out):
@@ -58,6 +50,7 @@ def tile_mla_pb_kernel(tc, x, wq_w, wq_b, cos, sin, out):
         x_pool = stack.enter_context(tc.tile_pool(name="x_pool", bufs=TOKEN_TILES))
         raw_pool = stack.enter_context(tc.tile_pool(name="raw_pool", bufs=BLOCKS_AHEAD * PASSES))
         grouped_pool = stack.enter_context(tc.tile_pool(name="grouped_pool", bufs=4))
+        first_pool = stack.enter_context(tc.tile_pool(name="first_pool", bufs=1))
         codes_pool = stack.enter_context(tc.tile_pool(name="codes_pool", bufs=6))
         q_pool = stack.enter_context(tc.tile_pool(name="q_pool", bufs=3))
         psum = stack.enter_context(tc.psum_pool(name="psum", bufs=8))
@@ -167,18 +160,25 @@ def tile_mla_pb_kernel(tc, x, wq_w, wq_b, cos, sin, out):
         acc = {}
 
         def regroup(u):
-            grouped = grouped_pool.tile([P, BANK, PACK], BF16, name="w_grouped", align_bytes=64)
-            split = BANK - vector_columns(u)
-            if split > 0:
-                nc.scalar.copy(
-                    out=grouped[:, 0:split, :].rearrange("p (c i) j -> p c j i", i=4),
-                    in_=w_raw[u][:, :, 0:split].rearrange("p j (c i) -> p c j i", i=4),
+            b, g = divmod(u, PASSES)
+            if g == 0:
+                grouped = first_pool.tile([P, BANK, PACK], BF16, name="w_first", align_bytes=64)
+                nc.gpsimd.tensor_scalar(
+                    out=grouped[:],
+                    in0=w_raw[u][:].rearrange("p j c -> p c j"),
+                    scalar1=1.0,
+                    scalar2=0.0,
+                    op0=MULT,
+                    op1=ADD,
                 )
-            if split < BANK:
-                nc.vector.tensor_copy(
-                    out=grouped[:, split:BANK, :].rearrange("p (c i) j -> p c j i", i=4),
-                    in_=w_raw[u][:, :, split:BANK].rearrange("p j (c i) -> p c j i", i=4),
-                )
+            else:
+                grouped = grouped_pool.tile([P, BANK, PACK], BF16, name="w_grouped", align_bytes=64)
+                dst = grouped[:].rearrange("p (c i) j -> p c j i", i=4)
+                src = w_raw[u][:].rearrange("p j (c i) -> p c j i", i=4)
+                if b == 0 and g % 2 == 1:
+                    nc.vector.tensor_copy(out=dst, in_=src)
+                else:
+                    nc.scalar.copy(out=dst, in_=src)
             w_grouped[u] = grouped
 
         def prepare(u):

@@ -33,6 +33,8 @@ Q_WIDTH = BANK + NOPE
 
 BLOCKS_AHEAD = 4
 
+GPSIMD_COLUMNS = 256
+
 FLOPS = 2 * TOKENS * DIM * COLS
 
 
@@ -163,13 +165,18 @@ def tile_mla_pb_kernel(tc, x, wq_w, wq_b, cos, sin, out):
             b, g = divmod(u, PASSES)
             if g == 0:
                 grouped = first_pool.tile([P, BANK, PACK], BF16, name="w_first", align_bytes=64)
+                split = BANK - GPSIMD_COLUMNS
                 nc.gpsimd.tensor_scalar(
-                    out=grouped[:],
-                    in0=w_raw[u][:].rearrange("p j c -> p c j"),
+                    out=grouped[:, split:BANK, :],
+                    in0=w_raw[u][:, :, split:BANK].rearrange("p j c -> p c j"),
                     scalar1=1.0,
                     scalar2=0.0,
                     op0=MULT,
                     op1=ADD,
+                )
+                nc.scalar.copy(
+                    out=grouped[:, 0:split, :].rearrange("p (c i) j -> p c j i", i=4),
+                    in_=w_raw[u][:, :, 0:split].rearrange("p j (c i) -> p c j i", i=4),
                 )
             else:
                 grouped = grouped_pool.tile([P, BANK, PACK], BF16, name="w_grouped", align_bytes=64)

@@ -22,24 +22,29 @@ ROPE = 64
 PAIRS = ROPE // 2
 COLS = 16 * HEAD
 BANK = 512
+PSUM_BANKS = 8
 
 TOKEN_TILES = TOKENS // P
 PASSES = DIM // K_PASS
-BLOCKS = COLS // BANK
-UNITS = BLOCKS * PASSES
+PANELS = COLS // BANK
+UNITS = PANELS * PASSES
 
 MAX_HEADS = 3
 Q_WIDTH = BANK + NOPE
 
-BLOCKS_AHEAD = 4
+PANELS_AHEAD = 4
+GROUPED_AHEAD = 4
+CODES_AHEAD = 6
+RESULT_TILES = 3
 
-GPSIMD_COLUMNS = 256
+GPSIMD_COLUMNS = 320
+RUN = 4
 
 FLOPS = 2 * TOKENS * DIM * COLS
 
 
-def first_column(b):
-    return (BLOCKS - 1 - b) * BANK
+def first_column(n):
+    return (PANELS - 1 - n) * BANK
 
 
 def tile_mla_pb_kernel(tc, x, wq_w, wq_b, cos, sin, out):
@@ -50,12 +55,12 @@ def tile_mla_pb_kernel(tc, x, wq_w, wq_b, cos, sin, out):
     with ExitStack() as stack:
         const = stack.enter_context(tc.tile_pool(name="const", bufs=1))
         x_pool = stack.enter_context(tc.tile_pool(name="x_pool", bufs=TOKEN_TILES))
-        raw_pool = stack.enter_context(tc.tile_pool(name="raw_pool", bufs=BLOCKS_AHEAD * PASSES))
-        grouped_pool = stack.enter_context(tc.tile_pool(name="grouped_pool", bufs=4))
+        raw_pool = stack.enter_context(tc.tile_pool(name="raw_pool", bufs=PANELS_AHEAD * PASSES))
+        grouped_pool = stack.enter_context(tc.tile_pool(name="grouped_pool", bufs=GROUPED_AHEAD))
         first_pool = stack.enter_context(tc.tile_pool(name="first_pool", bufs=1))
-        codes_pool = stack.enter_context(tc.tile_pool(name="codes_pool", bufs=6))
-        q_pool = stack.enter_context(tc.tile_pool(name="q_pool", bufs=3))
-        psum = stack.enter_context(tc.psum_pool(name="psum", bufs=8))
+        codes_pool = stack.enter_context(tc.tile_pool(name="codes_pool", bufs=CODES_AHEAD))
+        q_pool = stack.enter_context(tc.tile_pool(name="q_pool", bufs=RESULT_TILES))
+        psum = stack.enter_context(tc.psum_pool(name="psum", bufs=PSUM_BANKS))
 
         identity = const.tile([P, P], F32, name="identity")
         make_identity(nc, identity[:])
@@ -66,7 +71,7 @@ def tile_mla_pb_kernel(tc, x, wq_w, wq_b, cos, sin, out):
 
         w_raw = {}
 
-        def load_block(b):
+        def load_panel(n):
             for g in range(PASSES):
                 w_tile = raw_pool.tile([P, PACK, BANK], BF16, name="w_raw")
                 for u in range(2):
@@ -74,14 +79,14 @@ def tile_mla_pb_kernel(tc, x, wq_w, wq_b, cos, sin, out):
                     nc.sync.dma_start(
                         out=w_tile[:, 2 * u : 2 * u + 2, :],
                         in_=wq_w[
-                            first_row : first_row + 2 * P, first_column(b) : first_column(b) + BANK
+                            first_row : first_row + 2 * P, first_column(n) : first_column(n) + BANK
                         ].rearrange("(p e) c -> p e c", e=2),
                     )
-                w_raw[b * PASSES + g] = w_tile
+                w_raw[n * PASSES + g] = w_tile
 
         bias_rows = const.tile([P, BANK], BF16, name="bias_rows")
         nc.vector.memset(bias_rows[:].bitcast(F32), 0.0)
-        nc.sync.dma_start(out=bias_rows[0:BLOCKS, :], in_=wq_b.rearrange("(c n) -> c n", n=BANK))
+        nc.sync.dma_start(out=bias_rows[0:PANELS, :], in_=wq_b.rearrange("(c w) -> c w", w=BANK))
         cos_sb = const.tile([P, 2, PAIRS], BF16, name="cos_sb")
         sin_sb = const.tile([P, 2, PAIRS], BF16, name="sin_sb")
         nc.scalar.dma_start(out=cos_sb[:], in_=cos.rearrange("(a p) j -> p a j", p=P))
@@ -93,8 +98,8 @@ def tile_mla_pb_kernel(tc, x, wq_w, wq_b, cos, sin, out):
             nc.sync.dma_start(out=x_tile[:], in_=x_rows[t * P : (t + 1) * P, :])
             x_raw.append(x_tile)
 
-        for b in range(BLOCKS_AHEAD):
-            load_block(b)
+        for n in range(PANELS_AHEAD):
+            load_panel(n)
 
         bias_sb = const.tile([P, COLS], F32, name="bias_sb")
 
@@ -143,7 +148,7 @@ def tile_mla_pb_kernel(tc, x, wq_w, wq_b, cos, sin, out):
             x_scales.append(scales)
 
         for t in range(TOKEN_TILES):
-            for c in range(2 * t, min(2 * t + 2, BLOCKS)):
+            for c in range(2 * t, min(2 * t + 2, PANELS)):
                 spread_bias(c)
             x_flip(t)
             x_quantise(t)
@@ -162,7 +167,7 @@ def tile_mla_pb_kernel(tc, x, wq_w, wq_b, cos, sin, out):
         acc = {}
 
         def regroup(u):
-            b, g = divmod(u, PASSES)
+            n, g = divmod(u, PASSES)
             if g == 0:
                 grouped = first_pool.tile([P, BANK, PACK], BF16, name="w_first", align_bytes=64)
                 split = BANK - GPSIMD_COLUMNS
@@ -175,14 +180,14 @@ def tile_mla_pb_kernel(tc, x, wq_w, wq_b, cos, sin, out):
                     op1=ADD,
                 )
                 nc.scalar.copy(
-                    out=grouped[:, 0:split, :].rearrange("p (c i) j -> p c j i", i=4),
-                    in_=w_raw[u][:, :, 0:split].rearrange("p j (c i) -> p c j i", i=4),
+                    out=grouped[:, 0:split, :].rearrange("p (c i) j -> p c j i", i=RUN),
+                    in_=w_raw[u][:, :, 0:split].rearrange("p j (c i) -> p c j i", i=RUN),
                 )
             else:
                 grouped = grouped_pool.tile([P, BANK, PACK], BF16, name="w_grouped", align_bytes=64)
-                dst = grouped[:].rearrange("p (c i) j -> p c j i", i=4)
-                src = w_raw[u][:].rearrange("p j (c i) -> p c j i", i=4)
-                if b == 0 and g % 2 == 1:
+                dst = grouped[:].rearrange("p (c i) j -> p c j i", i=RUN)
+                src = w_raw[u][:].rearrange("p j (c i) -> p c j i", i=RUN)
+                if n == 0 and g % 2 == 1:
                     nc.vector.tensor_copy(out=dst, in_=src)
                 else:
                     nc.scalar.copy(out=dst, in_=src)
@@ -198,12 +203,12 @@ def tile_mla_pb_kernel(tc, x, wq_w, wq_b, cos, sin, out):
                 scales=scales[:],
                 in_=w_grouped[u][:].rearrange("p c j -> p (c j)"),
             )
-            b, g = divmod(u, PASSES)
+            n, g = divmod(u, PASSES)
             for t in range(TOKEN_TILES):
                 if g == 0:
-                    acc[(b, t)] = psum.tile([P, BANK], F32, name="acc", tag="bank")
+                    acc[(n, t)] = psum.tile([P, BANK], F32, name="acc", tag="bank")
                 nc.tensor.matmul_mx(
-                    out=acc[(b, t)][:],
+                    out=acc[(n, t)][:],
                     lhsT=x_codes[t][:, g * P : (g + 1) * P].bitcast(FP8X4),
                     lhsT_scale=x_scales[t][:, g * P : (g + 1) * P],
                     rhs=codes[:].bitcast(FP8X4),
@@ -215,27 +220,27 @@ def tile_mla_pb_kernel(tc, x, wq_w, wq_b, cos, sin, out):
         q_tiles = {}
         products = {}
 
-        def add_bias(b):
+        def add_bias(n):
             q_tile = q_pool.tile([P, TOKEN_TILES, Q_WIDTH], F32, name="q_tile")
             for t in range(TOKEN_TILES):
                 nc.vector.tensor_tensor(
                     out=q_tile[:, t, 0:BANK],
-                    in0=acc[(b, t)][:],
-                    in1=bias_sb[:, first_column(b) : first_column(b) + BANK],
+                    in0=acc[(n, t)][:],
+                    in1=bias_sb[:, first_column(n) : first_column(n) + BANK],
                     op=ADD,
                 )
-            q_tiles[b] = q_tile
+            q_tiles[n] = q_tile
 
-        def rotated_view(b):
-            first = (NOPE - first_column(b)) % HEAD
+        def rotated_view(n):
+            first = (NOPE - first_column(n)) % HEAD
             heads = (BANK - first + NOPE) // HEAD
-            view = q_tiles[b][:, :, first : first + heads * HEAD].rearrange(
+            view = q_tiles[n][:, :, first : first + heads * HEAD].rearrange(
                 "p (s a) (h d) -> p s a h d", a=2, d=HEAD
             )
             return heads, view[:, :, :, :, 0:ROPE].rearrange("p s a h (j e) -> p s a h j e", e=2)
 
-        def rotation_products(b):
-            heads, pairs = rotated_view(b)
+        def rotation_products(n):
+            heads, pairs = rotated_view(n)
             by_cos = q_pool.tile([P, 2, 2, MAX_HEADS, PAIRS, 2], F32, name="by_cos")
             by_sin = q_pool.tile([P, 2, 2, 2, MAX_HEADS, PAIRS], F32, name="by_sin")
             nc.vector.tensor_tensor(
@@ -253,11 +258,11 @@ def tile_mla_pb_kernel(tc, x, wq_w, wq_b, cos, sin, out):
                     .to_broadcast([P, 2, 2, heads, PAIRS]),
                     op=MULT,
                 )
-            products[b] = (by_cos, by_sin)
+            products[n] = (by_cos, by_sin)
 
-        def rotation_sum_and_store(b):
-            heads, pairs = rotated_view(b)
-            by_cos, by_sin = products[b]
+        def rotation_sum_and_store(n):
+            heads, pairs = rotated_view(n)
+            by_cos, by_sin = products[n]
             nc.vector.tensor_tensor(
                 out=pairs,
                 in0=by_cos[:, :, :, 0:heads],
@@ -265,26 +270,26 @@ def tile_mla_pb_kernel(tc, x, wq_w, wq_b, cos, sin, out):
                 op=ADD,
             )
             nc.sync.dma_start(
-                out=out_rows[:, first_column(b) : first_column(b) + BANK].rearrange(
+                out=out_rows[:, first_column(n) : first_column(n) + BANK].rearrange(
                     "(t p) c -> p t c", p=P
                 ),
-                in_=q_tiles[b][:, :, 0:BANK],
+                in_=q_tiles[n][:, :, 0:BANK],
             )
 
         regroup(0)
-        for b in range(BLOCKS + 1):
-            if 1 <= b and b - 1 + BLOCKS_AHEAD < BLOCKS:
-                load_block(b - 1 + BLOCKS_AHEAD)
-            if b < BLOCKS:
-                prepare(b * PASSES)
-            if b >= 1:
-                add_bias(b - 1)
-            if b < BLOCKS:
-                prepare(b * PASSES + 1)
-            if b >= 1:
-                rotation_products(b - 1)
-            if b < BLOCKS:
-                prepare(b * PASSES + 2)
-                prepare(b * PASSES + 3)
-            if b >= 1:
-                rotation_sum_and_store(b - 1)
+        for n in range(PANELS + 1):
+            if 1 <= n and n - 1 + PANELS_AHEAD < PANELS:
+                load_panel(n - 1 + PANELS_AHEAD)
+            if n < PANELS:
+                prepare(n * PASSES)
+            if n >= 1:
+                add_bias(n - 1)
+            if n < PANELS:
+                prepare(n * PASSES + 1)
+            if n >= 1:
+                rotation_products(n - 1)
+            if n < PANELS:
+                prepare(n * PASSES + 2)
+                prepare(n * PASSES + 3)
+            if n >= 1:
+                rotation_sum_and_store(n - 1)

from contextlib import ExitStack

import concourse.mybir as mybir
from concourse.masks import make_identity

F32 = mybir.dt.float32
BF16 = mybir.dt.bfloat16
U32 = mybir.dt.uint32
U8 = mybir.dt.uint8
FP8X4 = mybir.dt.float8_e4m3fn_x4
ADD = mybir.AluOpType.add
MULT = mybir.AluOpType.mult

P = 128
PACK = 4
K_PASS = P * PACK
TOKENS = 512
DIM = 2048
HEAD = 192
NOPE = 128
ROPE = 64
PAIRS = ROPE // 2
COLS = 16 * HEAD
BANK = 512
PSUM_BANKS = 8

TOKEN_TILES = TOKENS // P
PASSES = DIM // K_PASS
PANELS = COLS // BANK
UNITS = PANELS * PASSES

MAX_HEADS = 3
Q_WIDTH = BANK + NOPE

PANELS_AHEAD = 4
GROUPED_AHEAD = 4
CODES_AHEAD = 6
RESULT_TILES = 3

GPSIMD_COLUMNS = 320
RUN = 4

FLOPS = 2 * TOKENS * DIM * COLS


def first_column(n):
    return (PANELS - 1 - n) * BANK


def tile_mla_pb_kernel(tc, x, wq_w, wq_b, cos, sin, out):
    nc = tc.nc
    x_rows = x.flatten_outer_dims()
    out_rows = out.rearrange("b s h d -> (b s) (h d)")

    with ExitStack() as stack:
        const = stack.enter_context(tc.tile_pool(name="const", bufs=1))
        x_pool = stack.enter_context(tc.tile_pool(name="x_pool", bufs=TOKEN_TILES))
        raw_pool = stack.enter_context(tc.tile_pool(name="raw_pool", bufs=PANELS_AHEAD * PASSES))
        grouped_pool = stack.enter_context(tc.tile_pool(name="grouped_pool", bufs=GROUPED_AHEAD))
        first_pool = stack.enter_context(tc.tile_pool(name="first_pool", bufs=1))
        codes_pool = stack.enter_context(tc.tile_pool(name="codes_pool", bufs=CODES_AHEAD))
        q_pool = stack.enter_context(tc.tile_pool(name="q_pool", bufs=RESULT_TILES))
        psum = stack.enter_context(tc.psum_pool(name="psum", bufs=PSUM_BANKS))

        identity = const.tile([P, P], F32, name="identity")
        make_identity(nc, identity[:])
        identity_bf = const.tile([P, P], BF16, name="identity_bf")
        make_identity(nc, identity_bf[:])

        stack.enter_context(tc.manual_schedule())

        w_raw = {}

        def load_panel(n):
            for g in range(PASSES):
                w_tile = raw_pool.tile([P, PACK, BANK], BF16, name="w_raw")
                for u in range(2):
                    first_row = g * K_PASS + u * 2 * P
                    nc.sync.dma_start(
                        out=w_tile[:, 2 * u : 2 * u + 2, :],
                        in_=wq_w[
                            first_row : first_row + 2 * P, first_column(n) : first_column(n) + BANK
                        ].rearrange("(p e) c -> p e c", e=2),
                    )
                w_raw[n * PASSES + g] = w_tile

        bias_rows = const.tile([P, BANK], BF16, name="bias_rows")
        nc.vector.memset(bias_rows[:].bitcast(F32), 0.0)
        nc.sync.dma_start(out=bias_rows[0:PANELS, :], in_=wq_b.rearrange("(c w) -> c w", w=BANK))
        cos_sb = const.tile([P, 2, PAIRS], BF16, name="cos_sb")
        sin_sb = const.tile([P, 2, PAIRS], BF16, name="sin_sb")
        nc.scalar.dma_start(out=cos_sb[:], in_=cos.rearrange("(a p) j -> p a j", p=P))
        nc.scalar.dma_start(out=sin_sb[:], in_=sin.rearrange("(a p) j -> p a j", p=P))

        x_raw = []
        for t in range(TOKEN_TILES):
            x_tile = x_pool.tile([P, DIM], BF16, name="x_raw")
            nc.sync.dma_start(out=x_tile[:], in_=x_rows[t * P : (t + 1) * P, :])
            x_raw.append(x_tile)

        for n in range(PANELS_AHEAD):
            load_panel(n)

        bias_sb = const.tile([P, COLS], F32, name="bias_sb")

        def spread_bias(c):
            spread = psum.tile([P, BANK], F32, name="spread", tag="bank")
            nc.tensor.matmul(
                out=spread[:],
                lhsT=identity_bf[:, c : c + 1].to_broadcast([P, P]),
                rhs=bias_rows[:],
                start=True,
                stop=True,
            )
            nc.vector.tensor_copy(out=bias_sb[:, c * BANK : (c + 1) * BANK], in_=spread[:])

        x_grouped = []
        x_codes = []
        x_scales = []

        def x_flip(t):
            words = x_raw[t][:].bitcast(F32)
            grouped = x_pool.tile([P, PASSES * P * PACK], BF16, name="x_grouped", align_bytes=64)
            grouped_words = grouped[:].bitcast(F32).rearrange(
                "p (g r u) -> p g r u", g=PASSES, u=2
            )
            for half in range(2):
                flipped = psum.tile([P, 2, 2, P], F32, name="flipped", tag="bank")
                for gg in range(2):
                    for u in range(2):
                        first_word = ((2 * half + gg) * 2 + u) * P
                        nc.tensor.transpose(
                            flipped[:, gg, u, :], words[:, first_word : first_word + P], identity[:]
                        )
                nc.scalar.copy(
                    out=grouped_words[:, 2 * half : 2 * half + 2],
                    in_=flipped[:].rearrange("p g u r -> p g r u"),
                )
            x_grouped.append(grouped)

        def x_quantise(t):
            codes = x_pool.tile([P, PASSES * P], U32, name="x_codes", align_bytes=64)
            scales = x_pool.tile([P, PASSES * P], U8, name="x_scales", align_bytes=64)
            nc.vector.quantize_mx(
                out=codes[:].bitcast(FP8X4), scales=scales[:], in_=x_grouped[t][:]
            )
            x_codes.append(codes)
            x_scales.append(scales)

        for t in range(TOKEN_TILES):
            for c in range(2 * t, min(2 * t + 2, PANELS)):
                spread_bias(c)
            x_flip(t)
            x_quantise(t)

        cos_table = const.tile([P, 2, MAX_HEADS, PAIRS, 2], BF16, name="cos_table")
        sin_table = const.tile([P, 2, 2, MAX_HEADS, PAIRS], BF16, name="sin_table")
        nc.vector.tensor_copy(
            out=cos_table[:],
            in_=cos_sb[:].unsqueeze(2).unsqueeze(4).to_broadcast([P, 2, MAX_HEADS, PAIRS, 2]),
        )
        sin_heads = sin_sb[:].unsqueeze(2).to_broadcast([P, 2, MAX_HEADS, PAIRS])
        nc.vector.tensor_scalar_mul(out=sin_table[:, 0], in0=sin_heads, scalar1=-1.0)
        nc.vector.tensor_copy(out=sin_table[:, 1], in_=sin_heads)

        w_grouped = {}
        acc = {}

        def regroup(u):
            n, g = divmod(u, PASSES)
            if g == 0:
                grouped = first_pool.tile([P, BANK, PACK], BF16, name="w_first", align_bytes=64)
                split = BANK - GPSIMD_COLUMNS
                nc.gpsimd.tensor_scalar(
                    out=grouped[:, split:BANK, :],
                    in0=w_raw[u][:, :, split:BANK].rearrange("p j c -> p c j"),
                    scalar1=1.0,
                    scalar2=0.0,
                    op0=MULT,
                    op1=ADD,
                )
                nc.scalar.copy(
                    out=grouped[:, 0:split, :].rearrange("p (c i) j -> p c j i", i=RUN),
                    in_=w_raw[u][:, :, 0:split].rearrange("p j (c i) -> p c j i", i=RUN),
                )
            else:
                grouped = grouped_pool.tile([P, BANK, PACK], BF16, name="w_grouped", align_bytes=64)
                dst = grouped[:].rearrange("p (c i) j -> p c j i", i=RUN)
                src = w_raw[u][:].rearrange("p j (c i) -> p c j i", i=RUN)
                if n == 0 and g % 2 == 1:
                    nc.vector.tensor_copy(out=dst, in_=src)
                else:
                    nc.scalar.copy(out=dst, in_=src)
            w_grouped[u] = grouped

        def prepare(u):
            if u + 1 < UNITS:
                regroup(u + 1)
            codes = codes_pool.tile([P, BANK], U32, name="w_codes", align_bytes=64)
            scales = codes_pool.tile([P, BANK], U8, name="w_scales", align_bytes=64)
            nc.vector.quantize_mx(
                out=codes[:].bitcast(FP8X4),
                scales=scales[:],
                in_=w_grouped[u][:].rearrange("p c j -> p (c j)"),
            )
            n, g = divmod(u, PASSES)
            for t in range(TOKEN_TILES):
                if g == 0:
                    acc[(n, t)] = psum.tile([P, BANK], F32, name="acc", tag="bank")
                nc.tensor.matmul_mx(
                    out=acc[(n, t)][:],
                    lhsT=x_codes[t][:, g * P : (g + 1) * P].bitcast(FP8X4),
                    lhsT_scale=x_scales[t][:, g * P : (g + 1) * P],
                    rhs=codes[:].bitcast(FP8X4),
                    rhs_scale=scales[:],
                    start=(g == 0),
                    stop=(g == PASSES - 1),
                )

        q_tiles = {}
        products = {}

        def add_bias(n):
            q_tile = q_pool.tile([P, TOKEN_TILES, Q_WIDTH], F32, name="q_tile")
            for t in range(TOKEN_TILES):
                nc.vector.tensor_tensor(
                    out=q_tile[:, t, 0:BANK],
                    in0=acc[(n, t)][:],
                    in1=bias_sb[:, first_column(n) : first_column(n) + BANK],
                    op=ADD,
                )
            q_tiles[n] = q_tile

        def rotated_view(n):
            first = (NOPE - first_column(n)) % HEAD
            heads = (BANK - first + NOPE) // HEAD
            view = q_tiles[n][:, :, first : first + heads * HEAD].rearrange(
                "p (s a) (h d) -> p s a h d", a=2, d=HEAD
            )
            return heads, view[:, :, :, :, 0:ROPE].rearrange("p s a h (j e) -> p s a h j e", e=2)

        def rotation_products(n):
            heads, pairs = rotated_view(n)
            by_cos = q_pool.tile([P, 2, 2, MAX_HEADS, PAIRS, 2], F32, name="by_cos")
            by_sin = q_pool.tile([P, 2, 2, 2, MAX_HEADS, PAIRS], F32, name="by_sin")
            nc.vector.tensor_tensor(
                out=by_cos[:, :, :, 0:heads],
                in0=pairs,
                in1=cos_table[:, :, 0:heads].unsqueeze(1).to_broadcast([P, 2, 2, heads, PAIRS, 2]),
                op=MULT,
            )
            for e in range(2):
                nc.vector.tensor_tensor(
                    out=by_sin[:, e, :, :, 0:heads, :],
                    in0=pairs[:, :, :, :, :, 1 - e],
                    in1=sin_table[:, e, :, 0:heads, :]
                    .unsqueeze(1)
                    .to_broadcast([P, 2, 2, heads, PAIRS]),
                    op=MULT,
                )
            products[n] = (by_cos, by_sin)

        def rotation_sum_and_store(n):
            heads, pairs = rotated_view(n)
            by_cos, by_sin = products[n]
            nc.vector.tensor_tensor(
                out=pairs,
                in0=by_cos[:, :, :, 0:heads],
                in1=by_sin[:, :, :, :, 0:heads, :].rearrange("p e s a h j -> p s a h j e"),
                op=ADD,
            )
            nc.sync.dma_start(
                out=out_rows[:, first_column(n) : first_column(n) + BANK].rearrange(
                    "(t p) c -> p t c", p=P
                ),
                in_=q_tiles[n][:, :, 0:BANK],
            )

        regroup(0)
        for n in range(PANELS + 1):
            if 1 <= n and n - 1 + PANELS_AHEAD < PANELS:
                load_panel(n - 1 + PANELS_AHEAD)
            if n < PANELS:
                prepare(n * PASSES)
            if n >= 1:
                add_bias(n - 1)
            if n < PANELS:
                prepare(n * PASSES + 1)
            if n >= 1:
                rotation_products(n - 1)
            if n < PANELS:
                prepare(n * PASSES + 2)
                prepare(n * PASSES + 3)
            if n >= 1:
                rotation_sum_and_store(n - 1)
